import numpy as np
import ml_dtypes


def mxq(x, axis, fmt="e4m3"):
    dtype, down = {"e4m3": (ml_dtypes.float8_e4m3fn, 7), "e5m2": (ml_dtypes.float8_e5m2, 14)}[fmt]
    v = np.moveaxis(np.asarray(x, np.float32).astype(ml_dtypes.bfloat16).astype(np.float64), axis, -1)
    blocks = v.reshape(v.shape[:-1] + (-1, 32))
    amax = np.abs(blocks).max(-1, keepdims=True)
    byte = np.maximum(np.where(amax > 0, np.frexp(amax)[1] - 1 + 127, 0) - down, 1)
    scale = np.exp2(byte - 127.0)
    codes = (blocks / scale).astype(np.float32).astype(dtype).astype(np.float64)
    return np.moveaxis((codes * scale).reshape(v.shape), -1, axis)


WIDE = False


def mx_kscale(k):
    if not WIDE:
        return np.ones(k)
    levels = np.array([10, -10, 5, -5, 0])
    if k % 512:
        return np.exp2(np.random.permutation(np.resize(levels, k // 32))).repeat(32)
    a = np.empty((k // 512, 16))
    for p in range(k // 512):
        a[p, :8] = np.random.permutation(np.resize(levels, 8))
        for g in range(8):
            far = levels[np.abs(levels - a[p, g]) >= 10]
            a[p, g + 8] = far[np.random.randint(len(far))]
    return np.exp2(a.ravel()).repeat(32)


BF16 = ml_dtypes.bfloat16


def bf(x):
    return np.asarray(x, np.float32).astype(BF16)


def f64(x):
    return np.asarray(x).astype(np.float64)


S, HID, NH, Q_LORA, KV_LORA, NOPE, ROPE, VDIM, BLK = 2048, 4096, 16, 3072, 512, 128, 64, 128, 128
HEAD = NOPE + ROPE
EPS = 1e-6


def blockscale(rows, cols, k, g):
    return bf((np.random.random((rows, cols)) * 0.8 + 0.2) * g / np.sqrt(k))


def dequant(w, s):
    so = np.repeat(s, BLK, axis=0)[: w.shape[0]]
    se = np.repeat(so, BLK, axis=1)[:, : w.shape[1]]
    return w * se


def rmsnorm(x, w):
    var = np.mean(x * x, axis=-1, keepdims=True)
    return x * (1.0 / np.sqrt(var + EPS)) * w


def rotate_half(x):
    h = x.shape[-1] // 2
    return np.concatenate([-x[..., h:], x[..., :h]], axis=-1)


def setup_inputs():
    s, t = mx_kscale(HID), mx_kscale(Q_LORA)
    ang = np.arange(S)[:, None] / (10000.0 ** (np.arange(0, ROPE, 2) / ROPE))[None, :]
    ang = np.concatenate([ang, ang], axis=-1)
    return {"hidden_states": bf(np.random.standard_normal((S, HID)) * s),
            "cos": bf(np.cos(ang)),
            "sin": bf(np.sin(ang)),
            "wq_a": bf(np.random.standard_normal((Q_LORA, HID)) / s[None, :]),
            "sq_a": blockscale(Q_LORA // BLK, HID // BLK, HID, 1.0),
            "wq_b": bf(np.random.standard_normal((NH * HEAD, Q_LORA)) / t[None, :]),
            "sq_b": blockscale(NH * HEAD // BLK, Q_LORA // BLK, Q_LORA, 2.0),
            "q_ln_w": bf((1.0 + 0.1 * np.random.standard_normal(Q_LORA)) * t)}


def reference(hidden_states, cos, sin, wq_a, sq_a, wq_b, sq_b, q_ln_w):
    wa = dequant(f64(wq_a), f64(sq_a))
    lq = mxq(f64(hidden_states), 1, "e4m3") @ mxq(wa, 1, "e4m3").T
    h = rmsnorm(lq, f64(q_ln_w))
    wb = dequant(f64(wq_b), f64(sq_b))
    q = (mxq(h, 1, "e4m3") @ mxq(wb, 1, "e4m3").T).reshape(S, NH, HEAD)
    q_nope, q_pe = q[..., :NOPE], q[..., NOPE:]
    q_rot = q_pe * f64(cos)[:, None, :] + rotate_half(q_pe) * f64(sin)[:, None, :]
    return q_nope, q_rot

@@ -1,0 +1,543 @@
+from contextlib import ExitStack
+
+import concourse.mybir as mybir
+from concourse.masks import make_identity
+
+TOKENS, HIDDEN, LATENT, HEADS, NOPE, ROPE = 2048, 4096, 3072, 16, 128, 64
+HEAD = NOPE + ROPE
+EPS = 1e-6
+FLOPS = 2 * TOKENS * HIDDEN * LATENT + 2 * TOKENS * LATENT * HEADS * HEAD
+
+F32 = mybir.dt.float32
+BF16 = mybir.dt.bfloat16
+U32 = mybir.dt.uint32
+U8 = mybir.dt.uint8
+FP8X4 = mybir.dt.float8_e4m3fn_x4
+ALU = mybir.AluOpType
+ACT = mybir.ActivationFunctionType
+AXIS = mybir.AxisListType
+
+P = 128
+BLOCKS = TOKENS // P
+PASSES1 = HIDDEN // 512
+PASSES2 = LATENT // 512
+GROUPS = LATENT // 512
+HALF = ROPE // 2
+
+RAW_BUFS = 3
+GRP_BUFS = 3
+U_BUFS = 8
+HS_BUFS = 6
+TP_BUFS = 5
+ACC_BUFS = 3
+
+OUT_GROUPS = (("n", 0), ("r", 0), ("n", 1), ("n", 2), ("r", 1), ("n", 3))
+
+HEAD_ENGINES = ("S", "V", "S", "S", "S", "V", "S", "V")
+
+
+def tile_deepseekv3attention_pa_l_kernel(
+    tc, hidden_states, cos, sin, wq_a, sq_a, wq_b, sq_b, q_ln_w, out_0, out_1
+):
+    nc = tc.nc
+    with ExitStack() as ctx:
+        sb = ctx.enter_context(tc.tile_pool(name="sb", bufs=1))
+        ps = ctx.enter_context(tc.psum_pool(name="ps", bufs=1))
+        ctx.enter_context(tc.manual_schedule())
+
+        def tp_bank():
+            return ps.tile([P, 512], F32, tag="tp", bufs=TP_BUFS, name="tp")
+
+        def acc_bank():
+            return ps.tile([P, 512], F32, tag="acc", bufs=ACC_BUFS, name="acc")
+
+        def grp_tile():
+            return sb.tile([P, 2048], BF16, tag="grp", bufs=GRP_BUFS, name="grp", align_bytes=64)
+
+        def u_tile():
+            return sb.tile([P, 512], F32, tag="u", bufs=U_BUFS, name="u", align_bytes=64)
+
+        def small(name):
+            return sb.tile([P, 1], F32, tag=name, bufs=2, name=name)
+
+        stream = [("x", 0)]
+        stream.extend(("a", n) for n in range(12))
+        stream.append(("x", 1))
+        stream.extend(("a", n) for n in range(12, 24))
+        stream.extend(("x", b) for b in range(2, BLOCKS))
+        stream.extend(("b", q, c) for q in range(GROUPS) for c in range(3))
+        raw_tiles = {}
+        cursor = [0]
+        wq_b_heads = wq_b.rearrange("(h r) k -> r h k", r=HEAD)
+
+        def issue_load(i):
+            if i >= len(stream):
+                return
+            item = stream[i]
+            raw = sb.tile([P, 4096], BF16, tag="raw", bufs=RAW_BUFS, name="raw", align_bytes=64)
+            raw3 = raw[:].rearrange("p (j k) -> p j k", j=4)
+            if item[0] == "x":
+                b = item[1]
+                nc.sync.dma_start(out=raw[:], in_=hidden_states[b * P : (b + 1) * P, :])
+            elif item[0] == "a":
+                og, c = divmod(item[1], 4)
+                nc.sync.dma_start(
+                    out=raw3,
+                    in_=wq_a[512 * og : 512 * (og + 1), 1024 * c : 1024 * (c + 1)].rearrange(
+                        "(j p) k -> p j k", p=P
+                    ),
+                )
+            else:
+                kind, idx = OUT_GROUPS[item[1]]
+                cols = slice(1024 * item[2], 1024 * (item[2] + 1))
+                if kind == "n":
+                    nc.sync.dma_start(out=raw3, in_=wq_b_heads[0:NOPE, 4 * idx : 4 * idx + 4, cols])
+                else:
+                    for hh in range(2):
+                        nc.sync.dma_start(
+                            out=raw3[ROPE * hh : ROPE * (hh + 1), :, :],
+                            in_=wq_b_heads[NOPE:HEAD, 8 * idx + hh : 8 * idx + 8 : 2, cols],
+                        )
+            raw_tiles[i] = raw
+
+        def take(kind):
+            i = cursor[0]
+            assert stream[i][0] == kind
+            cursor[0] = i + 1
+            return raw_tiles[i]
+
+        def refill():
+            issue_load(cursor[0] - 1 + RAW_BUFS)
+
+        sq_pad = sb.tile([P, P], BF16, tag="sq_pad", name="sq_pad")
+        nc.vector.memset(sq_pad[:], 0.0)
+        nc.sync.dma_start(out=sq_pad[0:24, 0:32], in_=sq_a[:, :])
+        nc.sync.dma_start(out=sq_pad[0:24, 32:56], in_=sq_b[:, :])
+        for i in range(RAW_BUFS):
+            issue_load(i)
+        gain = sb.tile([P, LATENT], BF16, tag="gain", name="gain")
+        nc.sync.dma_start(out=gain[:], in_=q_ln_w.partition_broadcast(P))
+
+        warm_in = small("warm_in")
+        warm_out = small("warm_out")
+        nc.vector.memset(warm_in[:], 1.0)
+        nc.scalar.activation(out=warm_out[:], in_=warm_in[:], func=ACT.Sqrt)
+
+        ident_bf = sb.tile([P, P], BF16, tag="ident_bf", name="ident_bf")
+        make_identity(nc, ident_bf[:])
+        ident = sb.tile([P, P], F32, tag="ident", name="ident")
+        make_identity(nc, ident[:])
+
+        spread = grp_tile()
+        nc.vector.tensor_copy(
+            out=spread[:, 0:1792].rearrange("p (a c) -> p a c", c=32),
+            in_=ident_bf[:, 0:56].unsqueeze(2).to_broadcast([P, 56, 32]),
+        )
+        sq_ps = tp_bank()
+        nc.tensor.transpose(sq_ps[:].bitcast(BF16)[:, 0:P], sq_pad[:], ident_bf[:])
+        sq_t = sb.tile([P, 32], BF16, tag="sq_t", name="sq_t")
+        nc.vector.tensor_copy(out=sq_t[:], in_=sq_ps[:].bitcast(BF16)[:, 0:32])
+        fac_ps = tp_bank()
+        for i in range(PASSES1 + PASSES2):
+            nc.tensor.matmul(
+                fac_ps[:, 32 * i : 32 * (i + 1)],
+                lhsT=spread[:, P * i : P * (i + 1)],
+                rhs=sq_t[:],
+                start=True,
+                stop=True,
+            )
+        factors = sb.tile([P, 32 * (PASSES1 + PASSES2)], F32, tag="factors", name="factors")
+        nc.vector.tensor_copy(out=factors[:], in_=fac_ps[:, 0 : 32 * (PASSES1 + PASSES2)])
+
+        cos_t = sb.tile([P, BLOCKS, ROPE], BF16, tag="cos_t", name="cos_t")
+        sin_t = sb.tile([P, BLOCKS, ROPE], BF16, tag="sin_t", name="sin_t")
+
+        def load_rope_tables():
+            nc.sync.dma_start(out=cos_t[:], in_=cos.rearrange("(b p) d -> p b d", p=P))
+            nc.sync.dma_start(out=sin_t[:], in_=sin.rearrange("(b p) d -> p b d", p=P))
+            nc.vector.tensor_scalar(
+                out=sin_t[:, :, 0:HALF], in0=sin_t[:, :, 0:HALF], scalar1=-1.0, scalar2=None, op0=ALU.mult
+            )
+
+        pending = []
+
+        def flush_pending():
+            for quant in pending:
+                quant()
+            pending[:] = []
+
+        def run_halves(halves, engines):
+            halves[0][0](engines[0:2])
+            flush_pending()
+            halves[1][0](engines[2:4])
+            halves[0][1]()
+            pending.append(halves[1][1])
+
+        def copy_pairs(engine, bank, dst_words):
+            dst = dst_words.rearrange("p (g r u) -> p g r u", g=2, u=2)
+            src = bank[:].rearrange("p (g u r) -> p g r u", g=2, u=2)
+            if engine == "S":
+                nc.scalar.copy(out=dst, in_=src)
+            else:
+                nc.vector.tensor_copy(out=dst, in_=src)
+
+        x_codes = {}
+
+        def x_run(b):
+            raw = take("x")
+            words = raw[:].bitcast(F32)
+            banks = []
+            for i in range(4):
+                bank = tp_bank()
+                for gi in range(2):
+                    g = 2 * i + gi
+                    for u in range(2):
+                        s = 2 * gi + u
+                        nc.tensor.transpose(
+                            bank[:, P * s : P * (s + 1)], words[:, 256 * g + u : 256 * (g + 1) : 2], ident[:]
+                        )
+                banks.append(bank)
+            refill()
+            xc = sb.tile([P, 1024], U32, tag="xc", bufs=2, name="xc", align_bytes=64)
+            xp = sb.tile([P, 1024], U8, tag="xp", bufs=2, name="xp", align_bytes=64)
+            x_codes[b] = (xc, xp)
+
+            def half(t):
+                box = []
+
+                def evac(engines):
+                    grp = grp_tile()
+                    box.append(grp)
+                    gw = grp[:].bitcast(F32)
+                    for i in range(2):
+                        copy_pairs(engines[i], banks[2 * t + i], gw[:, 512 * i : 512 * (i + 1)])
+
+                def quant():
+                    nc.vector.quantize_mx(
+                        out=xc[:, 512 * t : 512 * (t + 1)].bitcast(FP8X4),
+                        scales=xp[:, 512 * t : 512 * (t + 1)],
+                        in_=box[0][:],
+                    )
+
+                return (evac, quant)
+
+            return (half(0), half(1))
+
+        def weight_run(kind, store, pass0, row0, blocks_of, on_quant):
+            raw = take(kind)
+            words = raw[:].bitcast(F32)
+            banks = []
+            for gi in range(2):
+                for jp in range(2):
+                    bank = tp_bank()
+                    for jj in range(2):
+                        base = 512 * (2 * jp + jj) + 256 * gi
+                        for u in range(2):
+                            s = 2 * jj + u
+                            nc.tensor.transpose(
+                                bank[:, P * s : P * (s + 1)], words[:, base + u : base + 256 : 2], ident[:]
+                            )
+                    banks.append(bank)
+            refill()
+
+            def half(gi):
+                g = pass0 + gi
+                box = []
+
+                def evac(engines):
+                    grp = grp_tile()
+                    box.append(grp)
+                    for jp in range(2):
+                        bank = banks[2 * gi + jp]
+                        for jj in range(2):
+                            j = 2 * jp + jj
+                            src = (
+                                bank[:, 256 * jj : 256 * (jj + 1)]
+                                .bitcast(BF16)
+                                .rearrange("p (u r e) -> p r u e", u=2, e=2)
+                            )
+                            dst = grp[:, 512 * j : 512 * (j + 1)].rearrange("p (r u e) -> p r u e", u=2, e=2)
+                            for r0, r1, ob in blocks_of(j):
+                                col = 32 * (row0 + g) + ob
+                                if engines[jp] == "S":
+                                    nc.scalar.activation(
+                                        out=dst[:, r0:r1],
+                                        in_=src[:, r0:r1],
+                                        func=ACT.Copy,
+                                        scale=factors[:, col : col + 1],
+                                    )
+                                else:
+                                    nc.vector.tensor_scalar(
+                                        out=dst[:, r0:r1],
+                                        in0=src[:, r0:r1],
+                                        scalar1=factors[:, col : col + 1],
+                                        scalar2=None,
+                                        op0=ALU.mult,
+                                    )
+
+                def quant():
+                    codes, planes = store()
+                    nc.vector.quantize_mx(
+                        out=codes[:, 512 * g : 512 * (g + 1)].bitcast(FP8X4),
+                        scales=planes[4 * (g % 4) : P, 512 * (g // 4) : 512 * (g // 4 + 1)],
+                        in_=box[0][:],
+                    )
+                    on_quant(g)
+
+                return (evac, quant)
+
+            return (half(0), half(1))
+
+        weights = {}
+
+        def weight_store(key):
+            def store():
+                if key not in weights:
+                    codes = sb.tile([P, 4096], U32, tag="wc", bufs=GROUPS, name="wc", align_bytes=64)
+                    planes = sb.tile([P, 1024], U8, tag="wp", bufs=GROUPS, name="wp", align_bytes=64)
+                    weights[key] = (codes, planes)
+                return weights[key]
+
+            return store
+
+        def wb_blocks(q):
+            kind, idx = OUT_GROUPS[q]
+
+            def blocks_of(j):
+                if kind == "n":
+                    first = HEAD * (4 * idx + j)
+                    obs = (first // P, (first + 64) // P)
+                else:
+                    obs = ((HEAD * (8 * idx + 2 * j) + NOPE) // P, (HEAD * (8 * idx + 2 * j + 1) + NOPE) // P)
+                if obs[0] == obs[1]:
+                    return ((0, P, obs[0]),)
+                return ((0, 64, obs[0]), (64, P, obs[1]))
+
+            return blocks_of
+
+        def wb_run(q, c):
+            return weight_run("b", weight_store(("b", q)), 2 * c, PASSES1, wb_blocks(q), lambda g: None)
+
+        def mx_pass(acc, lhs, rhs, g, last):
+            plane_rows = slice(4 * (g % 4), P)
+            if lhs[2]:
+                lhs_plane = lhs[1][plane_rows, P * (g // 4) : P * (g // 4 + 1)]
+            else:
+                lhs_plane = lhs[1][:, P * g : P * (g + 1)]
+            nc.tensor.matmul_mx(
+                out=acc[:],
+                lhsT=lhs[0][:, P * g : P * (g + 1)].bitcast(FP8X4),
+                lhsT_scale=lhs_plane,
+                rhs=rhs[0][:, 512 * g : 512 * (g + 1)].bitcast(FP8X4),
+                rhs_scale=rhs[1][plane_rows, 512 * (g // 4) : 512 * (g // 4 + 1)],
+                start=(g == 0),
+                stop=(g == last),
+            )
+
+        def stage1_pass(acc, b, og, g):
+            mx_pass(acc, (x_codes[b][0], x_codes[b][1], False), weights[("a", og)], g, PASSES1 - 1)
+
+        sums = {}
+        u_tiles = {}
+        rstd = {}
+        hs_tiles = {}
+        h_codes = {}
+
+        def close_stage1(b, og, acc):
+            if og == 0:
+                sums[b] = sb.tile([P, 8], F32, tag="sums", bufs=2, name="sums")
+            junk = sb.tile([P, 512], BF16, tag="junk", bufs=1, name="junk")
+            nc.scalar.activation(out=junk[:], in_=acc[:], func=ACT.Square, accum_out=sums[b][:, og : og + 1])
+            u = u_tile()
+            nc.vector.tensor_tensor(out=u[:], in0=acc[:], in1=gain[:, 512 * og : 512 * (og + 1)], op=ALU.mult)
+            u_tiles[(b, og)] = u
+
+        def scale_h(b, g):
+            hs = sb.tile([P, 512], BF16, tag="hs", bufs=HS_BUFS, name="hs", align_bytes=64)
+            nc.vector.tensor_scalar(
+                out=hs[:].rearrange("p (u m e) -> p u m e", u=2, e=2),
+                in0=u_tiles[(b, g)][:].rearrange("p (m u e) -> p u m e", u=2, e=2),
+                scalar1=rstd[b][:, 0:1],
+                scalar2=None,
+                op0=ALU.mult,
+            )
+            hs_tiles[(b, g)] = hs
+
+        def h_transposes(b):
+            banks = []
+            for i in range(3):
+                bank = tp_bank()
+                for gi in range(2):
+                    hw = hs_tiles[(b, 2 * i + gi)][:].bitcast(F32)
+                    for u in range(2):
+                        s = 2 * gi + u
+                        nc.tensor.transpose(bank[:, P * s : P * (s + 1)], hw[:, P * u : P * (u + 1)], ident[:])
+                banks.append(bank)
+            return banks
+
+        def h_evac(banks):
+            grps = []
+            for bank in banks:
+                grp = grp_tile()
+                copy_pairs("S", bank, grp[:, 0:1024].bitcast(F32))
+                grps.append(grp)
+            return grps
+
+        def h_quant(b, grps):
+            hc = sb.tile([P, P * PASSES2], U32, tag="hc%d" % b, name="hc%d" % b, align_bytes=64)
+            hp = sb.tile([P, 2 * P], U8, tag="hp%d" % b, name="hp%d" % b, align_bytes=64)
+            h_codes[b] = (hc, hp, True)
+            for g in range(PASSES2):
+                nc.vector.quantize_mx(
+                    out=hc[:, P * g : P * (g + 1)].bitcast(FP8X4),
+                    scales=hp[4 * (g % 4) : P, P * (g // 4) : P * (g // 4 + 1)],
+                    in_=grps[g // 2][:, 512 * (g % 2) : 512 * (g % 2 + 1)],
+                )
+
+        def block_end(b):
+            banks = h_transposes(b - 1) if b > 0 else None
+            total = small("total")
+            nc.vector.tensor_reduce(out=total[:], in_=sums[b][:, 0:GROUPS], axis=AXIS.X, op=ALU.add)
+            var = small("var")
+            nc.vector.tensor_scalar(
+                out=var[:], in0=total[:], scalar1=1.0 / LATENT, scalar2=EPS, op0=ALU.mult, op1=ALU.add
+            )
+            grps = h_evac(banks) if b > 0 else None
+            std = small("std")
+            nc.scalar.activation(out=std[:], in_=var[:], func=ACT.Sqrt)
+            if b > 0:
+                h_quant(b - 1, grps)
+            y0 = small("y0")
+            nc.vector.reciprocal(out=y0[:], in_=std[:])
+            t0 = small("t0")
+            nc.vector.scalar_tensor_tensor(
+                out=t0[:], in0=y0[:], scalar=var[:, 0:1], in1=y0[:], op0=ALU.mult, op1=ALU.mult
+            )
+            t1 = small("t1")
+            nc.vector.tensor_scalar(out=t1[:], in0=t0[:], scalar1=-0.5, scalar2=1.5, op0=ALU.mult, op1=ALU.add)
+            y = small("y")
+            nc.vector.tensor_tensor(out=y[:], in0=t1[:], in1=y0[:], op=ALU.mult)
+            rstd[b] = y
+
+        head_len = 26
+        ready = []
+        open_acc = {}
+        posts = []
+
+        def emit_ready(limit):
+            while ready and ready[0][0] <= limit:
+                og, g = ready[0][1], ready[0][2]
+                ready[:] = ready[1:]
+                if g == 0:
+                    open_acc[og] = acc_bank()
+                stage1_pass(open_acc[og], 0, og, g)
+                if g == PASSES1 - 1:
+                    posts.append(og)
+
+        def emit_posts():
+            for og in posts:
+                close_stage1(0, og, open_acc[og])
+            posts[:] = []
+
+        def wa_run(i, n):
+            og, c = divmod(n, 4)
+            return weight_run(
+                "a",
+                weight_store(("a", og)),
+                2 * c,
+                0,
+                lambda j: ((0, P, 4 * og + j),),
+                lambda g: ready.append((i, og, g)),
+            )
+
+        for i in range(head_len):
+            item = stream[i]
+            if item[0] == "x":
+                halves = x_run(item[1])
+                engines = ("S", "V", "S", "V")
+            else:
+                halves = wa_run(i, item[1])
+                engines = HEAD_ENGINES[4 * (i % 2) : 4 * (i % 2) + 4]
+            emit_ready(i - 2)
+            run_halves(halves, engines)
+            emit_posts()
+        flush_pending()
+        emit_ready(head_len)
+        emit_posts()
+        block_end(0)
+        load_rope_tables()
+
+        for b in range(1, BLOCKS):
+            for og in range(GROUPS):
+                acc = acc_bank()
+                for g in range(PASSES1):
+                    stage1_pass(acc, b, og, g)
+                close_stage1(b, og, acc)
+                if og < 3:
+                    scale_h(b - 1, 2 * og)
+                    scale_h(b - 1, 2 * og + 1)
+                if b + 1 < BLOCKS and og == 2:
+                    run_halves(x_run(b + 1), ("S", "S", "S", "S"))
+                    flush_pending()
+                if b + 1 == BLOCKS and og in (0, 1, 3):
+                    run_halves(wb_run(0, (0, 1, 3).index(og)), ("S", "V", "S", "S"))
+            flush_pending()
+            block_end(b)
+
+        last = BLOCKS - 1
+        for g in range(PASSES2):
+            scale_h(last, g)
+        delayed = {}
+        for q in range(GROUPS):
+            kind, idx = OUT_GROUPS[q]
+            for b in range(BLOCKS):
+                acc = acc_bank()
+                for g in range(PASSES2):
+                    mx_pass(acc, h_codes[b], weights[("b", q)], g, PASSES2 - 1)
+                rows = slice(b * P, (b + 1) * P)
+                if kind == "n":
+                    o = u_tile()
+                    nc.scalar.copy(out=o[:], in_=acc[:])
+                    nc.sync.dma_start(
+                        out=out_0[rows, 4 * idx : 4 * idx + 4, :], in_=o[:].rearrange("p (h d) -> p h d", d=NOPE)
+                    )
+                else:
+                    a3 = acc[:].rearrange("p (h d) -> p h d", d=ROPE)
+                    t1 = u_tile()
+                    t2 = u_tile()
+                    t13 = t1[:].rearrange("p (h d) -> p h d", d=ROPE)
+                    t23 = t2[:].rearrange("p (h d) -> p h d", d=ROPE)
+                    nc.vector.tensor_tensor(
+                        out=t13, in0=a3, in1=cos_t[:, b : b + 1, :].to_broadcast([P, 8, ROPE]), op=ALU.mult
+                    )
+                    nc.vector.tensor_tensor(
+                        out=t23[:, :, 0:HALF],
+                        in0=a3[:, :, HALF:ROPE],
+                        in1=sin_t[:, b : b + 1, 0:HALF].to_broadcast([P, 8, HALF]),
+                        op=ALU.mult,
+                    )
+                    nc.vector.tensor_tensor(
+                        out=t23[:, :, HALF:ROPE],
+                        in0=a3[:, :, 0:HALF],
+                        in1=sin_t[:, b : b + 1, HALF:ROPE].to_broadcast([P, 8, HALF]),
+                        op=ALU.mult,
+                    )
+                    nc.gpsimd.tensor_tensor(out=t1[:], in0=t1[:], in1=t2[:], op=ALU.add)
+                    nc.sync.dma_start(out=out_1[rows, 8 * idx : 8 * idx + 8, :], in_=t13)
+                for quant in delayed.get(b, ()):
+                    quant()
+                delayed[b] = ()
+                if q == 0 and b == 1:
+                    h_quant(last, h_evac(h_transposes(last)))
+                if q + 1 < GROUPS and b in (4, 8, 12):
+                    halves = wb_run(q + 1, (4, 8, 12).index(b))
+                    if kind == "n":
+                        halves[0][0](("V", "V"))
+                        halves[1][0](("V", "V"))
+                        halves[0][1]()
+                        halves[1][1]()
+                    else:
+                        halves[0][0](("S", "S"))
+                        halves[1][0](("S", "S"))
+                        delayed[b + 1] = (halves[0][1],)
+                        delayed[b + 2] = (halves[1][1],)

@@ -26,14 +26,15 @@ HALF = ROPE // 2
 
 RAW_BUFS = 3
 GRP_BUFS = 3
-U_BUFS = 8
+U_BUFS = 7
 HS_BUFS = 6
 TP_BUFS = 5
 ACC_BUFS = 3
 
 OUT_GROUPS = (("n", 0), ("r", 0), ("n", 1), ("n", 2), ("r", 1), ("n", 3))
-
 HEAD_ENGINES = ("S", "V", "S", "S", "S", "V", "S", "V")
+LATE_ENGINES = ("S", "V", "S", "S")
+WB_AT = (4, 8, 12)
 
 
 def tile_deepseekv3attention_pa_l_kernel(
@@ -44,6 +45,12 @@ def tile_deepseekv3attention_pa_l_kernel(
         sb = ctx.enter_context(tc.tile_pool(name="sb", bufs=1))
         ps = ctx.enter_context(tc.psum_pool(name="ps", bufs=1))
         ctx.enter_context(tc.manual_schedule())
+
+        def plane_rows(g):
+            return slice(4 * (2 * (g // 4) + g % 2), P)
+
+        def plane_cols(g, width):
+            return slice(width * ((g // 2) % 2), width * ((g // 2) % 2 + 1))
 
         def tp_bank():
             return ps.tile([P, 512], F32, tag="tp", bufs=TP_BUFS, name="tp")
@@ -60,10 +67,11 @@ def tile_deepseekv3attention_pa_l_kernel(
         def small(name):
             return sb.tile([P, 1], F32, tag=name, bufs=2, name=name)
 
-        stream = [("x", 0)]
-        stream.extend(("a", n) for n in range(12))
+        stream = [("a", 0), ("x", 0)]
+        stream.extend(("a", n) for n in range(1, 12))
         stream.append(("x", 1))
         stream.extend(("a", n) for n in range(12, 24))
+        head_len = len(stream)
         stream.extend(("x", b) for b in range(2, BLOCKS))
         stream.extend(("b", q, c) for q in range(GROUPS) for c in range(3))
         raw_tiles = {}
@@ -104,7 +112,7 @@ def tile_deepseekv3attention_pa_l_kernel(
             i = cursor[0]
             assert stream[i][0] == kind
             cursor[0] = i + 1
-            return raw_tiles[i]
+            return raw_tiles[i][:].bitcast(F32)
 
         def refill():
             issue_load(cursor[0] - 1 + RAW_BUFS)
@@ -149,15 +157,47 @@ def tile_deepseekv3attention_pa_l_kernel(
         factors = sb.tile([P, 32 * (PASSES1 + PASSES2)], F32, tag="factors", name="factors")
         nc.vector.tensor_copy(out=factors[:], in_=fac_ps[:, 0 : 32 * (PASSES1 + PASSES2)])
 
-        cos_t = sb.tile([P, BLOCKS, ROPE], BF16, tag="cos_t", name="cos_t")
-        sin_t = sb.tile([P, BLOCKS, ROPE], BF16, tag="sin_t", name="sin_t")
-
         def load_rope_tables():
-            nc.sync.dma_start(out=cos_t[:], in_=cos.rearrange("(b p) d -> p b d", p=P))
-            nc.sync.dma_start(out=sin_t[:], in_=sin.rearrange("(b p) d -> p b d", p=P))
+            tables = sb.tile([P, 2 * BLOCKS, ROPE], BF16, tag="gain", name="tables")
+            cos_t = tables[:, 0:BLOCKS, :]
+            sin_t = tables[:, BLOCKS : 2 * BLOCKS, :]
+            nc.sync.dma_start(out=cos_t, in_=cos.rearrange("(b p) d -> p b d", p=P))
+            nc.sync.dma_start(out=sin_t, in_=sin.rearrange("(b p) d -> p b d", p=P))
             nc.vector.tensor_scalar(
                 out=sin_t[:, :, 0:HALF], in0=sin_t[:, :, 0:HALF], scalar1=-1.0, scalar2=None, op0=ALU.mult
             )
+            return (cos_t, sin_t)
+
+        sorted_words = []
+
+        def sort_next(engine):
+            if cursor[0] >= len(stream) or stream[cursor[0]][0] == "a":
+                return
+            kind = stream[cursor[0]][0]
+            words = take(kind)
+            sorted_words[:] = []
+            for t in range(2):
+                if kind == "x":
+                    src = words[:, 1024 * t : 1024 * (t + 1)].rearrange("p (a w) -> p a w", a=4)
+                else:
+                    src = words.rearrange("p (a w) -> p a w", a=4)[:, :, 256 * t : 256 * (t + 1)]
+                xs = sb.tile([P, 2048], BF16, tag="xs", bufs=2, name="xs", align_bytes=64)
+                dst = xs[:].bitcast(F32).rearrange("p (a u m) -> p a u m", a=4, u=2)
+                if engine == "S":
+                    nc.scalar.copy(out=dst, in_=src.rearrange("p a (m u) -> p a u m", u=2))
+                else:
+                    nc.vector.tensor_copy(out=dst, in_=src.rearrange("p a (m u) -> p a u m", u=2))
+                sorted_words.append(xs[:].bitcast(F32))
+            refill()
+
+        def transposes(sources):
+            banks = []
+            for i in range(0, len(sources), 4):
+                bank = tp_bank()
+                for s in range(4):
+                    nc.tensor.transpose(bank[:, P * s : P * (s + 1)], sources[i + s], ident[:])
+                banks.append(bank)
+            return banks
 
         pending = []
 
@@ -166,12 +206,14 @@ def tile_deepseekv3attention_pa_l_kernel(
                 quant()
             pending[:] = []
 
-        def run_halves(halves, engines):
+        def run_halves(halves, engines, between=None):
             halves[0][0](engines[0:2])
             flush_pending()
+            made = between() if between is not None else None
             halves[1][0](engines[2:4])
             halves[0][1]()
             pending.append(halves[1][1])
+            return made
 
         def copy_pairs(engine, bank, dst_words):
             dst = dst_words.rearrange("p (g r u) -> p g r u", g=2, u=2)
@@ -184,23 +226,10 @@ def tile_deepseekv3attention_pa_l_kernel(
         x_codes = {}
 
         def x_run(b):
-            raw = take("x")
-            words = raw[:].bitcast(F32)
-            banks = []
-            for i in range(4):
-                bank = tp_bank()
-                for gi in range(2):
-                    g = 2 * i + gi
-                    for u in range(2):
-                        s = 2 * gi + u
-                        nc.tensor.transpose(
-                            bank[:, P * s : P * (s + 1)], words[:, 256 * g + u : 256 * (g + 1) : 2], ident[:]
-                        )
-                banks.append(bank)
-            refill()
+            banks = transposes([sorted_words[t][:, P * c : P * (c + 1)] for t in range(2) for c in range(8)])
             xc = sb.tile([P, 1024], U32, tag="xc", bufs=2, name="xc", align_bytes=64)
             xp = sb.tile([P, 1024], U8, tag="xp", bufs=2, name="xp", align_bytes=64)
-            x_codes[b] = (xc, xp)
+            x_codes[b] = (xc, xp, False)
 
             def half(t):
                 box = []
@@ -223,22 +252,10 @@ def tile_deepseekv3attention_pa_l_kernel(
 
             return (half(0), half(1))
 
-        def weight_run(kind, store, pass0, row0, blocks_of, on_quant):
-            raw = take(kind)
-            words = raw[:].bitcast(F32)
-            banks = []
-            for gi in range(2):
-                for jp in range(2):
-                    bank = tp_bank()
-                    for jj in range(2):
-                        base = 512 * (2 * jp + jj) + 256 * gi
-                        for u in range(2):
-                            s = 2 * jj + u
-                            nc.tensor.transpose(
-                                bank[:, P * s : P * (s + 1)], words[:, base + u : base + 256 : 2], ident[:]
-                            )
-                    banks.append(bank)
-            refill()
+        weights = {}
+
+        def weight_run(key, sources, pass0, row0, blocks_of, on_quant):
+            banks = transposes(sources)
 
             def half(gi):
                 g = pass0 + gi
@@ -247,39 +264,39 @@ def tile_deepseekv3attention_pa_l_kernel(
                 def evac(engines):
                     grp = grp_tile()
                     box.append(grp)
-                    for jp in range(2):
-                        bank = banks[2 * gi + jp]
-                        for jj in range(2):
-                            j = 2 * jp + jj
-                            src = (
-                                bank[:, 256 * jj : 256 * (jj + 1)]
-                                .bitcast(BF16)
-                                .rearrange("p (u r e) -> p r u e", u=2, e=2)
-                            )
-                            dst = grp[:, 512 * j : 512 * (j + 1)].rearrange("p (r u e) -> p r u e", u=2, e=2)
-                            for r0, r1, ob in blocks_of(j):
-                                col = 32 * (row0 + g) + ob
-                                if engines[jp] == "S":
-                                    nc.scalar.activation(
-                                        out=dst[:, r0:r1],
-                                        in_=src[:, r0:r1],
-                                        func=ACT.Copy,
-                                        scale=factors[:, col : col + 1],
-                                    )
-                                else:
-                                    nc.vector.tensor_scalar(
-                                        out=dst[:, r0:r1],
-                                        in0=src[:, r0:r1],
-                                        scalar1=factors[:, col : col + 1],
-                                        scalar2=None,
-                                        op0=ALU.mult,
-                                    )
+                    for j in range(4):
+                        src = (
+                            banks[2 * gi + j // 2][:, 256 * (j % 2) : 256 * (j % 2 + 1)]
+                            .bitcast(BF16)
+                            .rearrange("p (u r e) -> p r u e", u=2, e=2)
+                        )
+                        dst = grp[:, 512 * j : 512 * (j + 1)].rearrange("p (r u e) -> p r u e", u=2, e=2)
+                        for r0, r1, ob in blocks_of(j):
+                            col = 32 * (row0 + g) + ob
+                            if engines[j // 2] == "S":
+                                nc.scalar.activation(
+                                    out=dst[:, r0:r1],
+                                    in_=src[:, r0:r1],
+                                    func=ACT.Copy,
+                                    scale=factors[:, col : col + 1],
+                                )
+                            else:
+                                nc.vector.tensor_scalar(
+                                    out=dst[:, r0:r1],
+                                    in0=src[:, r0:r1],
+                                    scalar1=factors[:, col : col + 1],
+                                    scalar2=None,
+                                    op0=ALU.mult,
+                                )
 
                 def quant():
-                    codes, planes = store()
+                    if key not in weights:
+                        codes = sb.tile([P, 4096], U32, tag="wc", bufs=GROUPS, name="wc", align_bytes=64)
+                        planes = sb.tile([P, 1024], U8, tag="wp", bufs=GROUPS, name="wp", align_bytes=64)
+                        weights[key] = (codes, planes)
                     nc.vector.quantize_mx(
-                        out=codes[:, 512 * g : 512 * (g + 1)].bitcast(FP8X4),
-                        scales=planes[4 * (g % 4) : P, 512 * (g // 4) : 512 * (g // 4 + 1)],
+                        out=weights[key][0][:, 512 * g : 512 * (g + 1)].bitcast(FP8X4),
+                        scales=weights[key][1][plane_rows(g), plane_cols(g, 512)],
                         in_=box[0][:],
                     )
                     on_quant(g)
@@ -287,18 +304,6 @@ def tile_deepseekv3attention_pa_l_kernel(
                 return (evac, quant)
 
             return (half(0), half(1))
-
-        weights = {}
-
-        def weight_store(key):
-            def store():
-                if key not in weights:
-                    codes = sb.tile([P, 4096], U32, tag="wc", bufs=GROUPS, name="wc", align_bytes=64)
-                    planes = sb.tile([P, 1024], U8, tag="wp", bufs=GROUPS, name="wp", align_bytes=64)
-                    weights[key] = (codes, planes)
-                return weights[key]
-
-            return store
 
         def wb_blocks(q):
             kind, idx = OUT_GROUPS[q]
@@ -316,12 +321,12 @@ def tile_deepseekv3attention_pa_l_kernel(
             return blocks_of
 
         def wb_run(q, c):
-            return weight_run("b", weight_store(("b", q)), 2 * c, PASSES1, wb_blocks(q), lambda g: None)
+            sources = [sorted_words[gi][:, P * s : P * (s + 1)] for gi in range(2) for s in range(8)]
+            return weight_run(("b", q), sources, 2 * c, PASSES1, wb_blocks(q), lambda g: None)
 
         def mx_pass(acc, lhs, rhs, g, last):
-            plane_rows = slice(4 * (g % 4), P)
             if lhs[2]:
-                lhs_plane = lhs[1][plane_rows, P * (g // 4) : P * (g // 4 + 1)]
+                lhs_plane = lhs[1][plane_rows(g), plane_cols(g, P)]
             else:
                 lhs_plane = lhs[1][:, P * g : P * (g + 1)]
             nc.tensor.matmul_mx(
@@ -329,13 +334,10 @@ def tile_deepseekv3attention_pa_l_kernel(
                 lhsT=lhs[0][:, P * g : P * (g + 1)].bitcast(FP8X4),
                 lhsT_scale=lhs_plane,
                 rhs=rhs[0][:, 512 * g : 512 * (g + 1)].bitcast(FP8X4),
-                rhs_scale=rhs[1][plane_rows, 512 * (g // 4) : 512 * (g // 4 + 1)],
+                rhs_scale=rhs[1][plane_rows(g), plane_cols(g, 512)],
                 start=(g == 0),
                 stop=(g == last),
             )
-
-        def stage1_pass(acc, b, og, g):
-            mx_pass(acc, (x_codes[b][0], x_codes[b][1], False), weights[("a", og)], g, PASSES1 - 1)
 
         sums = {}
         u_tiles = {}
@@ -364,49 +366,35 @@ def tile_deepseekv3attention_pa_l_kernel(
             hs_tiles[(b, g)] = hs
 
         def h_transposes(b):
-            banks = []
-            for i in range(3):
-                bank = tp_bank()
-                for gi in range(2):
-                    hw = hs_tiles[(b, 2 * i + gi)][:].bitcast(F32)
-                    for u in range(2):
-                        s = 2 * gi + u
-                        nc.tensor.transpose(bank[:, P * s : P * (s + 1)], hw[:, P * u : P * (u + 1)], ident[:])
-                banks.append(bank)
-            return banks
+            return transposes(
+                [hs_tiles[(b, g)][:].bitcast(F32)[:, P * u : P * (u + 1)] for g in range(PASSES2) for u in range(2)]
+            )
 
-        def h_evac(banks):
-            grps = []
-            for bank in banks:
-                grp = grp_tile()
-                copy_pairs("S", bank, grp[:, 0:1024].bitcast(F32))
-                grps.append(grp)
-            return grps
-
-        def h_quant(b, grps):
+        def h_finish(b, banks):
             hc = sb.tile([P, P * PASSES2], U32, tag="hc%d" % b, name="hc%d" % b, align_bytes=64)
             hp = sb.tile([P, 2 * P], U8, tag="hp%d" % b, name="hp%d" % b, align_bytes=64)
             h_codes[b] = (hc, hp, True)
-            for g in range(PASSES2):
-                nc.vector.quantize_mx(
-                    out=hc[:, P * g : P * (g + 1)].bitcast(FP8X4),
-                    scales=hp[4 * (g % 4) : P, P * (g // 4) : P * (g // 4 + 1)],
-                    in_=grps[g // 2][:, 512 * (g % 2) : 512 * (g % 2 + 1)],
-                )
+            for i in range(3):
+                grp = grp_tile()
+                copy_pairs("S", banks[i], grp[:, 0:1024].bitcast(F32))
+                if i == 0:
+                    flush_pending()
+                for g in (2 * i, 2 * i + 1):
+                    nc.vector.quantize_mx(
+                        out=hc[:, P * g : P * (g + 1)].bitcast(FP8X4),
+                        scales=hp[plane_rows(g), plane_cols(g, P)],
+                        in_=grp[:, 512 * (g % 2) : 512 * (g % 2 + 1)],
+                    )
 
-        def block_end(b):
-            banks = h_transposes(b - 1) if b > 0 else None
+        def norm_factor(b):
             total = small("total")
             nc.vector.tensor_reduce(out=total[:], in_=sums[b][:, 0:GROUPS], axis=AXIS.X, op=ALU.add)
             var = small("var")
             nc.vector.tensor_scalar(
                 out=var[:], in0=total[:], scalar1=1.0 / LATENT, scalar2=EPS, op0=ALU.mult, op1=ALU.add
             )
-            grps = h_evac(banks) if b > 0 else None
             std = small("std")
             nc.scalar.activation(out=std[:], in_=var[:], func=ACT.Sqrt)
-            if b > 0:
-                h_quant(b - 1, grps)
             y0 = small("y0")
             nc.vector.reciprocal(out=y0[:], in_=std[:])
             t0 = small("t0")
@@ -419,7 +407,6 @@ def tile_deepseekv3attention_pa_l_kernel(
             nc.vector.tensor_tensor(out=y[:], in0=t1[:], in1=y0[:], op=ALU.mult)
             rstd[b] = y
 
-        head_len = 26
         ready = []
         open_acc = {}
         posts = []
@@ -430,7 +417,7 @@ def tile_deepseekv3attention_pa_l_kernel(
                 ready[:] = ready[1:]
                 if g == 0:
                     open_acc[og] = acc_bank()
-                stage1_pass(open_acc[og], 0, og, g)
+                mx_pass(open_acc[og], x_codes[0], weights[("a", og)], g, PASSES1 - 1)
                 if g == PASSES1 - 1:
                     posts.append(og)
 
@@ -441,50 +428,80 @@ def tile_deepseekv3attention_pa_l_kernel(
 
         def wa_run(i, n):
             og, c = divmod(n, 4)
-            return weight_run(
-                "a",
-                weight_store(("a", og)),
-                2 * c,
-                0,
-                lambda j: ((0, P, 4 * og + j),),
-                lambda g: ready.append((i, og, g)),
+            words = take("a")
+            sources = [
+                words[:, 512 * j + 256 * gi + u : 512 * j + 256 * (gi + 1) : 2]
+                for gi in range(2)
+                for j in range(4)
+                for u in range(2)
+            ]
+            halves = weight_run(
+                ("a", og), sources, 2 * c, 0, lambda j: ((0, P, 4 * og + j),), lambda g: ready.append((i, og, g))
             )
+            refill()
+            return halves
 
+        def stage1_group(b, og):
+            acc = acc_bank()
+            for g in range(PASSES1):
+                mx_pass(acc, x_codes[b], weights[("a", og)], g, PASSES1 - 1)
+            close_stage1(b, og, acc)
+
+        runs = []
         for i in range(head_len):
-            item = stream[i]
-            if item[0] == "x":
-                halves = x_run(item[1])
+            if stream[i][0] == "a":
+                runs.append(("a", stream[i][1]))
+                if i > 0 and stream[i - 1][0] == "x":
+                    runs.append(stream[i - 1])
+        for r in range(len(runs)):
+            if runs[r][0] == "x":
+                halves = x_run(runs[r][1])
                 engines = ("S", "V", "S", "V")
             else:
-                halves = wa_run(i, item[1])
-                engines = HEAD_ENGINES[4 * (i % 2) : 4 * (i % 2) + 4]
-            emit_ready(i - 2)
+                halves = wa_run(r, runs[r][1])
+                engines = HEAD_ENGINES[4 * (r % 2) : 4 * (r % 2) + 4]
+            if r >= 4:
+                emit_ready(r - 2)
             run_halves(halves, engines)
             emit_posts()
+            sort_next("V")
+        stage1_group(1, 0)
         flush_pending()
-        emit_ready(head_len)
+        emit_ready(len(runs))
         emit_posts()
-        block_end(0)
-        load_rope_tables()
+        norm_factor(0)
 
+        last = BLOCKS - 1
         for b in range(1, BLOCKS):
             for og in range(GROUPS):
-                acc = acc_bank()
-                for g in range(PASSES1):
-                    stage1_pass(acc, b, og, g)
-                close_stage1(b, og, acc)
+                if b > 1 or og > 0:
+                    stage1_group(b, og)
+                flush_pending()
                 if og < 3:
                     scale_h(b - 1, 2 * og)
                     scale_h(b - 1, 2 * og + 1)
-                if b + 1 < BLOCKS and og == 2:
-                    run_halves(x_run(b + 1), ("S", "S", "S", "S"))
-                    flush_pending()
-                if b + 1 == BLOCKS and og in (0, 1, 3):
-                    run_halves(wb_run(0, (0, 1, 3).index(og)), ("S", "V", "S", "S"))
-            flush_pending()
-            block_end(b)
+                if b == last - 1 and og == GROUPS - 1:
+                    halves = wb_run(0, 0)
+                    halves[0][0](LATE_ENGINES[0:2])
+                    halves[1][0](LATE_ENGINES[2:4])
+                    pending.extend((halves[0][1], halves[1][1]))
+                    sort_next("S")
+                if b == last and og == 1:
+                    run_halves(wb_run(0, 1), LATE_ENGINES)
+                    sort_next("S")
+                if og == 3:
+                    if b < last:
+                        halves = x_run(b + 1)
+                        engines = ("S", "S", "S", "S")
+                    else:
+                        halves = wb_run(0, 2)
+                        engines = LATE_ENGINES
+                    banks = run_halves(halves, engines, lambda: h_transposes(b - 1))
+                    h_finish(b - 1, banks)
+                    sort_next("V" if b + 1 < last else "S")
+            norm_factor(b)
+        cos_t, sin_t = load_rope_tables()
 
-        last = BLOCKS - 1
         for g in range(PASSES2):
             scale_h(last, g)
         delayed = {}
@@ -527,17 +544,22 @@ def tile_deepseekv3attention_pa_l_kernel(
                 for quant in delayed.get(b, ()):
                     quant()
                 delayed[b] = ()
-                if q == 0 and b == 1:
-                    h_quant(last, h_evac(h_transposes(last)))
-                if q + 1 < GROUPS and b in (4, 8, 12):
-                    halves = wb_run(q + 1, (4, 8, 12).index(b))
+                if q + 1 < GROUPS and b in WB_AT:
+                    halves = wb_run(q + 1, WB_AT.index(b))
+                    banks = None
                     if kind == "n":
                         halves[0][0](("V", "V"))
+                        if q == 0 and b == WB_AT[0]:
+                            banks = h_transposes(last)
                         halves[1][0](("V", "V"))
                         halves[0][1]()
                         halves[1][1]()
+                        sort_next("V")
                     else:
                         halves[0][0](("S", "S"))
                         halves[1][0](("S", "S"))
                         delayed[b + 1] = (halves[0][1],)
                         delayed[b + 2] = (halves[1][1],)
+                        sort_next("S")
+                    if banks is not None:
+                        h_finish(last, banks)

@@ -33,8 +33,9 @@ ACC_BUFS = 3
 
 OUT_GROUPS = (("n", 0), ("r", 0), ("n", 1), ("n", 2), ("r", 1), ("n", 3))
 HEAD_ENGINES = ("S", "V", "S", "S", "S", "V", "S", "V")
-LATE_ENGINES = ("S", "V", "S", "S")
-WB_AT = (4, 8, 12)
+LATE_ENGINES = ("V", "V", "S", "V")
+WB_AT = (3, 7, 11)
+MID = 4
 
 
 def tile_deepseekv3attention_pa_l_kernel(
@@ -170,7 +171,7 @@ def tile_deepseekv3attention_pa_l_kernel(
 
         sorted_words = []
 
-        def sort_next(engine):
+        def sort_next(engine, refill_now=True):
             if cursor[0] >= len(stream) or stream[cursor[0]][0] == "a":
                 return
             kind = stream[cursor[0]][0]
@@ -188,7 +189,8 @@ def tile_deepseekv3attention_pa_l_kernel(
                 else:
                     nc.vector.tensor_copy(out=dst, in_=src.rearrange("p a (m u) -> p a u m", u=2))
                 sorted_words.append(xs[:].bitcast(F32))
-            refill()
+            if refill_now:
+                refill()
 
         def transposes(sources):
             banks = []
@@ -356,12 +358,13 @@ def tile_deepseekv3attention_pa_l_kernel(
 
         def scale_h(b, g):
             hs = sb.tile([P, 512], BF16, tag="hs", bufs=HS_BUFS, name="hs", align_bytes=64)
-            nc.vector.tensor_scalar(
+            nc.gpsimd.tensor_scalar(
                 out=hs[:].rearrange("p (u m e) -> p u m e", u=2, e=2),
                 in0=u_tiles[(b, g)][:].rearrange("p (m u e) -> p u m e", u=2, e=2),
                 scalar1=rstd[b][:, 0:1],
-                scalar2=None,
+                scalar2=0.0,
                 op0=ALU.mult,
+                op1=ALU.add,
             )
             hs_tiles[(b, g)] = hs
 
@@ -406,6 +409,8 @@ def tile_deepseekv3attention_pa_l_kernel(
             y = small("y")
             nc.vector.tensor_tensor(out=y[:], in0=t1[:], in1=y0[:], op=ALU.mult)
             rstd[b] = y
+            for g in range(PASSES2):
+                scale_h(b, g)
 
         ready = []
         open_acc = {}
@@ -477,33 +482,29 @@ def tile_deepseekv3attention_pa_l_kernel(
                 if b > 1 or og > 0:
                     stage1_group(b, og)
                 flush_pending()
-                if og < 3:
-                    scale_h(b - 1, 2 * og)
-                    scale_h(b - 1, 2 * og + 1)
                 if b == last - 1 and og == GROUPS - 1:
                     halves = wb_run(0, 0)
+                    sort_next("S")
                     halves[0][0](LATE_ENGINES[0:2])
                     halves[1][0](LATE_ENGINES[2:4])
                     pending.extend((halves[0][1], halves[1][1]))
-                    sort_next("S")
                 if b == last and og == 1:
-                    run_halves(wb_run(0, 1), LATE_ENGINES)
+                    halves = wb_run(0, 1)
                     sort_next("S")
-                if og == 3:
+                    run_halves(halves, LATE_ENGINES)
+                if og == (MID if b < last else MID - 1):
                     if b < last:
                         halves = x_run(b + 1)
-                        engines = ("S", "S", "S", "S")
+                        engines = ("S", "V", "S", "V")
                     else:
                         halves = wb_run(0, 2)
                         engines = LATE_ENGINES
                     banks = run_halves(halves, engines, lambda: h_transposes(b - 1))
                     h_finish(b - 1, banks)
-                    sort_next("V" if b + 1 < last else "S")
+                    sort_next("S")
             norm_factor(b)
         cos_t, sin_t = load_rope_tables()
 
-        for g in range(PASSES2):
-            scale_h(last, g)
         delayed = {}
         for q in range(GROUPS):
             kind, idx = OUT_GROUPS[q]
@@ -544,6 +545,8 @@ def tile_deepseekv3attention_pa_l_kernel(
                 for quant in delayed.get(b, ()):
                     quant()
                 delayed[b] = ()
+                if q + 1 < GROUPS and b - 3 in WB_AT:
+                    refill()
                 if q + 1 < GROUPS and b in WB_AT:
                     halves = wb_run(q + 1, WB_AT.index(b))
                     banks = None
@@ -554,12 +557,12 @@ def tile_deepseekv3attention_pa_l_kernel(
                         halves[1][0](("V", "V"))
                         halves[0][1]()
                         halves[1][1]()
-                        sort_next("V")
+                        delayed[b + 1] = (lambda: sort_next("S", False),)
                     else:
                         halves[0][0](("S", "S"))
                         halves[1][0](("S", "S"))
                         delayed[b + 1] = (halves[0][1],)
                         delayed[b + 2] = (halves[1][1],)
-                        sort_next("S")
+                        sort_next("S", False)
                     if banks is not None:
                         h_finish(last, banks)

@@ -24,7 +24,7 @@ PASSES2 = LATENT // 512
 GROUPS = LATENT // 512
 HALF = ROPE // 2
 
-RAW_BUFS = 3
+RAW_BUFS = 4
 GRP_BUFS = 3
 U_BUFS = 7
 HS_BUFS = 6
@@ -68,10 +68,10 @@ def tile_deepseekv3attention_pa_l_kernel(
         def small(name):
             return sb.tile([P, 1], F32, tag=name, bufs=2, name=name)
 
-        stream = [("a", 0), ("x", 0)]
-        stream.extend(("a", n) for n in range(1, 12))
+        stream = [("a", 0), ("a", 1), ("a", 2), ("x", 0)]
+        stream.extend(("a", n) for n in range(3, 14))
         stream.append(("x", 1))
-        stream.extend(("a", n) for n in range(12, 24))
+        stream.extend(("a", n) for n in range(14, 24))
         head_len = len(stream)
         stream.extend(("x", b) for b in range(2, BLOCKS))
         stream.extend(("b", q, c) for q in range(GROUPS) for c in range(3))
@@ -90,12 +90,12 @@ def tile_deepseekv3attention_pa_l_kernel(
                 nc.sync.dma_start(out=raw[:], in_=hidden_states[b * P : (b + 1) * P, :])
             elif item[0] == "a":
                 og, c = divmod(item[1], 4)
-                nc.sync.dma_start(
-                    out=raw3,
-                    in_=wq_a[512 * og : 512 * (og + 1), 1024 * c : 1024 * (c + 1)].rearrange(
-                        "(j p) k -> p j k", p=P
-                    ),
-                )
+                rows = wq_a[512 * og : 512 * (og + 1), 1024 * c : 1024 * (c + 1)].rearrange("(j p) k -> p j k", p=P)
+                if i == 0:
+                    for j in range(4):
+                        nc.sync.dma_start(out=raw3[:, j : j + 1, :], in_=rows[:, j : j + 1, :])
+                else:
+                    nc.sync.dma_start(out=raw3, in_=rows)
             else:
                 kind, idx = OUT_GROUPS[item[1]]
                 cols = slice(1024 * item[2], 1024 * (item[2] + 1))
@@ -169,28 +169,8 @@ def tile_deepseekv3attention_pa_l_kernel(
             )
             return (cos_t, sin_t)
 
-        sorted_words = []
-
-        def sort_next(engine, refill_now=True):
-            if cursor[0] >= len(stream) or stream[cursor[0]][0] == "a":
-                return
-            kind = stream[cursor[0]][0]
-            words = take(kind)
-            sorted_words[:] = []
-            for t in range(2):
-                if kind == "x":
-                    src = words[:, 1024 * t : 1024 * (t + 1)].rearrange("p (a w) -> p a w", a=4)
-                else:
-                    src = words.rearrange("p (a w) -> p a w", a=4)[:, :, 256 * t : 256 * (t + 1)]
-                xs = sb.tile([P, 2048], BF16, tag="xs", bufs=2, name="xs", align_bytes=64)
-                dst = xs[:].bitcast(F32).rearrange("p (a u m) -> p a u m", a=4, u=2)
-                if engine == "S":
-                    nc.scalar.copy(out=dst, in_=src.rearrange("p a (m u) -> p a u m", u=2))
-                else:
-                    nc.vector.tensor_copy(out=dst, in_=src.rearrange("p a (m u) -> p a u m", u=2))
-                sorted_words.append(xs[:].bitcast(F32))
-            if refill_now:
-                refill()
+        def every_2nd_word(words, base):
+            return [words[:, base + u : base + 256 : 2] for u in range(2)]
 
         def transposes(sources):
             banks = []
@@ -228,7 +208,9 @@ def tile_deepseekv3attention_pa_l_kernel(
         x_codes = {}
 
         def x_run(b):
-            banks = transposes([sorted_words[t][:, P * c : P * (c + 1)] for t in range(2) for c in range(8)])
+            words = take("x")
+            banks = transposes([src for g in range(PASSES1) for src in every_2nd_word(words, 256 * g)])
+            refill()
             xc = sb.tile([P, 1024], U32, tag="xc", bufs=2, name="xc", align_bytes=64)
             xp = sb.tile([P, 1024], U8, tag="xp", bufs=2, name="xp", align_bytes=64)
             x_codes[b] = (xc, xp, False)
@@ -307,6 +289,9 @@ def tile_deepseekv3attention_pa_l_kernel(
 
             return (half(0), half(1))
 
+        def chunk_sources(words):
+            return [src for gi in range(2) for j in range(4) for src in every_2nd_word(words, 512 * j + 256 * gi)]
+
         def wb_blocks(q):
             kind, idx = OUT_GROUPS[q]
 
@@ -323,8 +308,9 @@ def tile_deepseekv3attention_pa_l_kernel(
             return blocks_of
 
         def wb_run(q, c):
-            sources = [sorted_words[gi][:, P * s : P * (s + 1)] for gi in range(2) for s in range(8)]
-            return weight_run(("b", q), sources, 2 * c, PASSES1, wb_blocks(q), lambda g: None)
+            halves = weight_run(("b", q), chunk_sources(take("b")), 2 * c, PASSES1, wb_blocks(q), lambda g: None)
+            refill()
+            return halves
 
         def mx_pass(acc, lhs, rhs, g, last):
             if lhs[2]:
@@ -433,15 +419,13 @@ def tile_deepseekv3attention_pa_l_kernel(
 
         def wa_run(i, n):
             og, c = divmod(n, 4)
-            words = take("a")
-            sources = [
-                words[:, 512 * j + 256 * gi + u : 512 * j + 256 * (gi + 1) : 2]
-                for gi in range(2)
-                for j in range(4)
-                for u in range(2)
-            ]
             halves = weight_run(
-                ("a", og), sources, 2 * c, 0, lambda j: ((0, P, 4 * og + j),), lambda g: ready.append((i, og, g))
+                ("a", og),
+                chunk_sources(take("a")),
+                2 * c,
+                0,
+                lambda j: ((0, P, 4 * og + j),),
+                lambda g: ready.append((i, og, g)),
             )
             refill()
             return halves
@@ -452,12 +436,7 @@ def tile_deepseekv3attention_pa_l_kernel(
                 mx_pass(acc, x_codes[b], weights[("a", og)], g, PASSES1 - 1)
             close_stage1(b, og, acc)
 
-        runs = []
-        for i in range(head_len):
-            if stream[i][0] == "a":
-                runs.append(("a", stream[i][1]))
-                if i > 0 and stream[i - 1][0] == "x":
-                    runs.append(stream[i - 1])
+        runs = stream[0:head_len]
         for r in range(len(runs)):
             if runs[r][0] == "x":
                 halves = x_run(runs[r][1])
@@ -465,11 +444,10 @@ def tile_deepseekv3attention_pa_l_kernel(
             else:
                 halves = wa_run(r, runs[r][1])
                 engines = HEAD_ENGINES[4 * (r % 2) : 4 * (r % 2) + 4]
-            if r >= 4:
+            if r >= 5:
                 emit_ready(r - 2)
             run_halves(halves, engines)
             emit_posts()
-            sort_next("V")
         stage1_group(1, 0)
         flush_pending()
         emit_ready(len(runs))
@@ -484,14 +462,11 @@ def tile_deepseekv3attention_pa_l_kernel(
                 flush_pending()
                 if b == last - 1 and og == GROUPS - 1:
                     halves = wb_run(0, 0)
-                    sort_next("S")
                     halves[0][0](LATE_ENGINES[0:2])
                     halves[1][0](LATE_ENGINES[2:4])
                     pending.extend((halves[0][1], halves[1][1]))
                 if b == last and og == 1:
-                    halves = wb_run(0, 1)
-                    sort_next("S")
-                    run_halves(halves, LATE_ENGINES)
+                    run_halves(wb_run(0, 1), LATE_ENGINES)
                 if og == (MID if b < last else MID - 1):
                     if b < last:
                         halves = x_run(b + 1)
@@ -501,7 +476,6 @@ def tile_deepseekv3attention_pa_l_kernel(
                         engines = LATE_ENGINES
                     banks = run_halves(halves, engines, lambda: h_transposes(b - 1))
                     h_finish(b - 1, banks)
-                    sort_next("S")
             norm_factor(b)
         cos_t, sin_t = load_rope_tables()
 
@@ -545,8 +519,6 @@ def tile_deepseekv3attention_pa_l_kernel(
                 for quant in delayed.get(b, ()):
                     quant()
                 delayed[b] = ()
-                if q + 1 < GROUPS and b - 3 in WB_AT:
-                    refill()
                 if q + 1 < GROUPS and b in WB_AT:
                     halves = wb_run(q + 1, WB_AT.index(b))
                     banks = None
@@ -557,12 +529,10 @@ def tile_deepseekv3attention_pa_l_kernel(
                         halves[1][0](("V", "V"))
                         halves[0][1]()
                         halves[1][1]()
-                        delayed[b + 1] = (lambda: sort_next("S", False),)
                     else:
                         halves[0][0](("S", "S"))
                         halves[1][0](("S", "S"))
                         delayed[b + 1] = (halves[0][1],)
                         delayed[b + 2] = (halves[1][1],)
-                        sort_next("S", False)
                     if banks is not None:
                         h_finish(last, banks)

from contextlib import ExitStack

import concourse.mybir as mybir
from concourse.masks import make_identity

TOKENS, HIDDEN, LATENT, HEADS, NOPE, ROPE = 2048, 4096, 3072, 16, 128, 64
HEAD = NOPE + ROPE
EPS = 1e-6
FLOPS = 2 * TOKENS * HIDDEN * LATENT + 2 * TOKENS * LATENT * HEADS * HEAD

F32 = mybir.dt.float32
BF16 = mybir.dt.bfloat16
U32 = mybir.dt.uint32
U8 = mybir.dt.uint8
FP8X4 = mybir.dt.float8_e4m3fn_x4
ALU = mybir.AluOpType
ACT = mybir.ActivationFunctionType
AXIS = mybir.AxisListType

P = 128
BLOCKS = TOKENS // P
PASSES1 = HIDDEN // 512
PASSES2 = LATENT // 512
GROUPS = LATENT // 512
HALF = ROPE // 2

RAW_BUFS = 4
GRP_BUFS = 3
U_BUFS = 7
HS_BUFS = 6
TP_BUFS = 5
ACC_BUFS = 3

OUT_GROUPS = (("n", 0), ("r", 0), ("n", 1), ("n", 2), ("r", 1), ("n", 3))
HEAD_ENGINES = ("S", "V", "S", "S", "S", "V", "S", "V")
LATE_ENGINES = ("V", "V", "S", "V")
WB_AT = (3, 7, 11)
MID = 4


def tile_deepseekv3attention_pa_l_kernel(
    tc, hidden_states, cos, sin, wq_a, sq_a, wq_b, sq_b, q_ln_w, out_0, out_1
):
    nc = tc.nc
    with ExitStack() as ctx:
        sb = ctx.enter_context(tc.tile_pool(name="sb", bufs=1))
        ps = ctx.enter_context(tc.psum_pool(name="ps", bufs=1))
        ctx.enter_context(tc.manual_schedule())

        def plane_rows(g):
            return slice(4 * (2 * (g // 4) + g % 2), P)

        def plane_cols(g, width):
            return slice(width * ((g // 2) % 2), width * ((g // 2) % 2 + 1))

        def tp_bank():
            return ps.tile([P, 512], F32, tag="tp", bufs=TP_BUFS, name="tp")

        def acc_bank():
            return ps.tile([P, 512], F32, tag="acc", bufs=ACC_BUFS, name="acc")

        def grp_tile():
            return sb.tile([P, 2048], BF16, tag="grp", bufs=GRP_BUFS, name="grp", align_bytes=64)

        def u_tile():
            return sb.tile([P, 512], F32, tag="u", bufs=U_BUFS, name="u", align_bytes=64)

        def small(name):
            return sb.tile([P, 1], F32, tag=name, bufs=2, name=name)

        stream = [("a", 0), ("a", 1), ("a", 2), ("x", 0)]
        stream.extend(("a", n) for n in range(3, 14))
        stream.append(("x", 1))
        stream.extend(("a", n) for n in range(14, 24))
        head_len = len(stream)
        stream.extend(("x", b) for b in range(2, BLOCKS))
        stream.extend(("b", q, c) for q in range(GROUPS) for c in range(3))
        raw_tiles = {}
        cursor = [0]
        wq_b_heads = wq_b.rearrange("(h r) k -> r h k", r=HEAD)

        def issue_load(i):
            if i >= len(stream):
                return
            item = stream[i]
            raw = sb.tile([P, 4096], BF16, tag="raw", bufs=RAW_BUFS, name="raw", align_bytes=64)
            raw3 = raw[:].rearrange("p (j k) -> p j k", j=4)
            if item[0] == "x":
                b = item[1]
                nc.sync.dma_start(out=raw[:], in_=hidden_states[b * P : (b + 1) * P, :])
            elif item[0] == "a":
                og, c = divmod(item[1], 4)
                rows = wq_a[512 * og : 512 * (og + 1), 1024 * c : 1024 * (c + 1)].rearrange("(j p) k -> p j k", p=P)
                if i == 0:
                    for j in range(4):
                        nc.sync.dma_start(out=raw3[:, j : j + 1, :], in_=rows[:, j : j + 1, :])
                else:
                    nc.sync.dma_start(out=raw3, in_=rows)
            else:
                kind, idx = OUT_GROUPS[item[1]]
                cols = slice(1024 * item[2], 1024 * (item[2] + 1))
                if kind == "n":
                    nc.sync.dma_start(out=raw3, in_=wq_b_heads[0:NOPE, 4 * idx : 4 * idx + 4, cols])
                else:
                    for hh in range(2):
                        nc.sync.dma_start(
                            out=raw3[ROPE * hh : ROPE * (hh + 1), :, :],
                            in_=wq_b_heads[NOPE:HEAD, 8 * idx + hh : 8 * idx + 8 : 2, cols],
                        )
            raw_tiles[i] = raw

        def take(kind):
            i = cursor[0]
            assert stream[i][0] == kind
            cursor[0] = i + 1
            return raw_tiles[i][:].bitcast(F32)

        def refill():
            issue_load(cursor[0] - 1 + RAW_BUFS)

        sq_pad = sb.tile([P, P], BF16, tag="sq_pad", name="sq_pad")
        nc.vector.memset(sq_pad[:], 0.0)
        nc.sync.dma_start(out=sq_pad[0:24, 0:32], in_=sq_a[:, :])
        nc.sync.dma_start(out=sq_pad[0:24, 32:56], in_=sq_b[:, :])
        for i in range(RAW_BUFS):
            issue_load(i)
        gain = sb.tile([P, LATENT], BF16, tag="gain", name="gain")
        nc.sync.dma_start(out=gain[:], in_=q_ln_w.partition_broadcast(P))

        warm_in = small("warm_in")
        warm_out = small("warm_out")
        nc.vector.memset(warm_in[:], 1.0)
        nc.scalar.activation(out=warm_out[:], in_=warm_in[:], func=ACT.Sqrt)

        ident_bf = sb.tile([P, P], BF16, tag="ident_bf", name="ident_bf")
        make_identity(nc, ident_bf[:])
        ident = sb.tile([P, P], F32, tag="ident", name="ident")
        make_identity(nc, ident[:])

        spread = grp_tile()
        nc.vector.tensor_copy(
            out=spread[:, 0:1792].rearrange("p (a c) -> p a c", c=32),
            in_=ident_bf[:, 0:56].unsqueeze(2).to_broadcast([P, 56, 32]),
        )
        sq_ps = tp_bank()
        nc.tensor.transpose(sq_ps[:].bitcast(BF16)[:, 0:P], sq_pad[:], ident_bf[:])
        sq_t = sb.tile([P, 32], BF16, tag="sq_t", name="sq_t")
        nc.vector.tensor_copy(out=sq_t[:], in_=sq_ps[:].bitcast(BF16)[:, 0:32])
        fac_ps = tp_bank()
        for i in range(PASSES1 + PASSES2):
            nc.tensor.matmul(
                fac_ps[:, 32 * i : 32 * (i + 1)],
                lhsT=spread[:, P * i : P * (i + 1)],
                rhs=sq_t[:],
                start=True,
                stop=True,
            )
        factors = sb.tile([P, 32 * (PASSES1 + PASSES2)], F32, tag="factors", name="factors")
        nc.vector.tensor_copy(out=factors[:], in_=fac_ps[:, 0 : 32 * (PASSES1 + PASSES2)])

        def load_rope_tables():
            tables = sb.tile([P, 2 * BLOCKS, ROPE], BF16, tag="gain", name="tables")
            cos_t = tables[:, 0:BLOCKS, :]
            sin_t = tables[:, BLOCKS : 2 * BLOCKS, :]
            nc.sync.dma_start(out=cos_t, in_=cos.rearrange("(b p) d -> p b d", p=P))
            nc.sync.dma_start(out=sin_t, in_=sin.rearrange("(b p) d -> p b d", p=P))
            nc.vector.tensor_scalar(
                out=sin_t[:, :, 0:HALF], in0=sin_t[:, :, 0:HALF], scalar1=-1.0, scalar2=None, op0=ALU.mult
            )
            return (cos_t, sin_t)

        def every_2nd_word(words, base):
            return [words[:, base + u : base + 256 : 2] for u in range(2)]

        def transposes(sources):
            banks = []
            for i in range(0, len(sources), 4):
                bank = tp_bank()
                for s in range(4):
                    nc.tensor.transpose(bank[:, P * s : P * (s + 1)], sources[i + s], ident[:])
                banks.append(bank)
            return banks

        pending = []

        def flush_pending():
            for quant in pending:
                quant()
            pending[:] = []

        def run_halves(halves, engines, between=None):
            halves[0][0](engines[0:2])
            flush_pending()
            made = between() if between is not None else None
            halves[1][0](engines[2:4])
            halves[0][1]()
            pending.append(halves[1][1])
            return made

        def copy_pairs(engine, bank, dst_words):
            dst = dst_words.rearrange("p (g r u) -> p g r u", g=2, u=2)
            src = bank[:].rearrange("p (g u r) -> p g r u", g=2, u=2)
            if engine == "S":
                nc.scalar.copy(out=dst, in_=src)
            else:
                nc.vector.tensor_copy(out=dst, in_=src)

        x_codes = {}

        def x_run(b):
            words = take("x")
            banks = transposes([src for g in range(PASSES1) for src in every_2nd_word(words, 256 * g)])
            refill()
            xc = sb.tile([P, 1024], U32, tag="xc", bufs=2, name="xc", align_bytes=64)
            xp = sb.tile([P, 1024], U8, tag="xp", bufs=2, name="xp", align_bytes=64)
            x_codes[b] = (xc, xp, False)

            def half(t):
                box = []

                def evac(engines):
                    grp = grp_tile()
                    box.append(grp)
                    gw = grp[:].bitcast(F32)
                    for i in range(2):
                        copy_pairs(engines[i], banks[2 * t + i], gw[:, 512 * i : 512 * (i + 1)])

                def quant():
                    nc.vector.quantize_mx(
                        out=xc[:, 512 * t : 512 * (t + 1)].bitcast(FP8X4),
                        scales=xp[:, 512 * t : 512 * (t + 1)],
                        in_=box[0][:],
                    )

                return (evac, quant)

            return (half(0), half(1))

        weights = {}

        def weight_run(key, sources, pass0, row0, blocks_of, on_quant):
            banks = transposes(sources)

            def half(gi):
                g = pass0 + gi
                box = []

                def evac(engines):
                    grp = grp_tile()
                    box.append(grp)
                    for j in range(4):
                        src = (
                            banks[2 * gi + j // 2][:, 256 * (j % 2) : 256 * (j % 2 + 1)]
                            .bitcast(BF16)
                            .rearrange("p (u r e) -> p r u e", u=2, e=2)
                        )
                        dst = grp[:, 512 * j : 512 * (j + 1)].rearrange("p (r u e) -> p r u e", u=2, e=2)
                        for r0, r1, ob in blocks_of(j):
                            col = 32 * (row0 + g) + ob
                            if engines[j // 2] == "S":
                                nc.scalar.activation(
                                    out=dst[:, r0:r1],
                                    in_=src[:, r0:r1],
                                    func=ACT.Copy,
                                    scale=factors[:, col : col + 1],
                                )
                            else:
                                nc.vector.tensor_scalar(
                                    out=dst[:, r0:r1],
                                    in0=src[:, r0:r1],
                                    scalar1=factors[:, col : col + 1],
                                    scalar2=None,
                                    op0=ALU.mult,
                                )

                def quant():
                    if key not in weights:
                        codes = sb.tile([P, 4096], U32, tag="wc", bufs=GROUPS, name="wc", align_bytes=64)
                        planes = sb.tile([P, 1024], U8, tag="wp", bufs=GROUPS, name="wp", align_bytes=64)
                        weights[key] = (codes, planes)
                    nc.vector.quantize_mx(
                        out=weights[key][0][:, 512 * g : 512 * (g + 1)].bitcast(FP8X4),
                        scales=weights[key][1][plane_rows(g), plane_cols(g, 512)],
                        in_=box[0][:],
                    )
                    on_quant(g)

                return (evac, quant)

            return (half(0), half(1))

        def chunk_sources(words):
            return [src for gi in range(2) for j in range(4) for src in every_2nd_word(words, 512 * j + 256 * gi)]

        def wb_blocks(q):
            kind, idx = OUT_GROUPS[q]

            def blocks_of(j):
                if kind == "n":
                    first = HEAD * (4 * idx + j)
                    obs = (first // P, (first + 64) // P)
                else:
                    obs = ((HEAD * (8 * idx + 2 * j) + NOPE) // P, (HEAD * (8 * idx + 2 * j + 1) + NOPE) // P)
                if obs[0] == obs[1]:
                    return ((0, P, obs[0]),)
                return ((0, 64, obs[0]), (64, P, obs[1]))

            return blocks_of

        def wb_run(q, c):
            halves = weight_run(("b", q), chunk_sources(take("b")), 2 * c, PASSES1, wb_blocks(q), lambda g: None)
            refill()
            return halves

        def mx_pass(acc, lhs, rhs, g, last):
            if lhs[2]:
                lhs_plane = lhs[1][plane_rows(g), plane_cols(g, P)]
            else:
                lhs_plane = lhs[1][:, P * g : P * (g + 1)]
            nc.tensor.matmul_mx(
                out=acc[:],
                lhsT=lhs[0][:, P * g : P * (g + 1)].bitcast(FP8X4),
                lhsT_scale=lhs_plane,
                rhs=rhs[0][:, 512 * g : 512 * (g + 1)].bitcast(FP8X4),
                rhs_scale=rhs[1][plane_rows(g), plane_cols(g, 512)],
                start=(g == 0),
                stop=(g == last),
            )

        sums = {}
        u_tiles = {}
        rstd = {}
        hs_tiles = {}
        h_codes = {}

        def close_stage1(b, og, acc):
            if og == 0:
                sums[b] = sb.tile([P, 8], F32, tag="sums", bufs=2, name="sums")
            junk = sb.tile([P, 512], BF16, tag="junk", bufs=1, name="junk")
            nc.scalar.activation(out=junk[:], in_=acc[:], func=ACT.Square, accum_out=sums[b][:, og : og + 1])
            u = u_tile()
            nc.vector.tensor_tensor(out=u[:], in0=acc[:], in1=gain[:, 512 * og : 512 * (og + 1)], op=ALU.mult)
            u_tiles[(b, og)] = u

        def scale_h(b, g):
            hs = sb.tile([P, 512], BF16, tag="hs", bufs=HS_BUFS, name="hs", align_bytes=64)
            nc.gpsimd.tensor_scalar(
                out=hs[:].rearrange("p (u m e) -> p u m e", u=2, e=2),
                in0=u_tiles[(b, g)][:].rearrange("p (m u e) -> p u m e", u=2, e=2),
                scalar1=rstd[b][:, 0:1],
                scalar2=0.0,
                op0=ALU.mult,
                op1=ALU.add,
            )
            hs_tiles[(b, g)] = hs

        def h_transposes(b):
            return transposes(
                [hs_tiles[(b, g)][:].bitcast(F32)[:, P * u : P * (u + 1)] for g in range(PASSES2) for u in range(2)]
            )

        def h_finish(b, banks):
            hc = sb.tile([P, P * PASSES2], U32, tag="hc%d" % b, name="hc%d" % b, align_bytes=64)
            hp = sb.tile([P, 2 * P], U8, tag="hp%d" % b, name="hp%d" % b, align_bytes=64)
            h_codes[b] = (hc, hp, True)
            for i in range(3):
                grp = grp_tile()
                copy_pairs("S", banks[i], grp[:, 0:1024].bitcast(F32))
                if i == 0:
                    flush_pending()
                for g in (2 * i, 2 * i + 1):
                    nc.vector.quantize_mx(
                        out=hc[:, P * g : P * (g + 1)].bitcast(FP8X4),
                        scales=hp[plane_rows(g), plane_cols(g, P)],
                        in_=grp[:, 512 * (g % 2) : 512 * (g % 2 + 1)],
                    )

        def norm_factor(b):
            total = small("total")
            nc.vector.tensor_reduce(out=total[:], in_=sums[b][:, 0:GROUPS], axis=AXIS.X, op=ALU.add)
            var = small("var")
            nc.vector.tensor_scalar(
                out=var[:], in0=total[:], scalar1=1.0 / LATENT, scalar2=EPS, op0=ALU.mult, op1=ALU.add
            )
            std = small("std")
            nc.scalar.activation(out=std[:], in_=var[:], func=ACT.Sqrt)
            y0 = small("y0")
            nc.vector.reciprocal(out=y0[:], in_=std[:])
            t0 = small("t0")
            nc.vector.scalar_tensor_tensor(
                out=t0[:], in0=y0[:], scalar=var[:, 0:1], in1=y0[:], op0=ALU.mult, op1=ALU.mult
            )
            t1 = small("t1")
            nc.vector.tensor_scalar(out=t1[:], in0=t0[:], scalar1=-0.5, scalar2=1.5, op0=ALU.mult, op1=ALU.add)
            y = small("y")
            nc.vector.tensor_tensor(out=y[:], in0=t1[:], in1=y0[:], op=ALU.mult)
            rstd[b] = y
            for g in range(PASSES2):
                scale_h(b, g)

        ready = []
        open_acc = {}
        posts = []

        def emit_ready(limit):
            while ready and ready[0][0] <= limit:
                og, g = ready[0][1], ready[0][2]
                ready[:] = ready[1:]
                if g == 0:
                    open_acc[og] = acc_bank()
                mx_pass(open_acc[og], x_codes[0], weights[("a", og)], g, PASSES1 - 1)
                if g == PASSES1 - 1:
                    posts.append(og)

        def emit_posts():
            for og in posts:
                close_stage1(0, og, open_acc[og])
            posts[:] = []

        def wa_run(i, n):
            og, c = divmod(n, 4)
            halves = weight_run(
                ("a", og),
                chunk_sources(take("a")),
                2 * c,
                0,
                lambda j: ((0, P, 4 * og + j),),
                lambda g: ready.append((i, og, g)),
            )
            refill()
            return halves

        def stage1_group(b, og):
            acc = acc_bank()
            for g in range(PASSES1):
                mx_pass(acc, x_codes[b], weights[("a", og)], g, PASSES1 - 1)
            close_stage1(b, og, acc)

        runs = stream[0:head_len]
        for r in range(len(runs)):
            if runs[r][0] == "x":
                halves = x_run(runs[r][1])
                engines = ("S", "V", "S", "V")
            else:
                halves = wa_run(r, runs[r][1])
                engines = HEAD_ENGINES[4 * (r % 2) : 4 * (r % 2) + 4]
            if r >= 5:
                emit_ready(r - 2)
            run_halves(halves, engines)
            emit_posts()
        stage1_group(1, 0)
        flush_pending()
        emit_ready(len(runs))
        emit_posts()
        norm_factor(0)

        last = BLOCKS - 1
        for b in range(1, BLOCKS):
            for og in range(GROUPS):
                if b > 1 or og > 0:
                    stage1_group(b, og)
                flush_pending()
                if b == last - 1 and og == GROUPS - 1:
                    halves = wb_run(0, 0)
                    halves[0][0](LATE_ENGINES[0:2])
                    halves[1][0](LATE_ENGINES[2:4])
                    pending.extend((halves[0][1], halves[1][1]))
                if b == last and og == 1:
                    run_halves(wb_run(0, 1), LATE_ENGINES)
                if og == (MID if b < last else MID - 1):
                    if b < last:
                        halves = x_run(b + 1)
                        engines = ("S", "V", "S", "V")
                    else:
                        halves = wb_run(0, 2)
                        engines = LATE_ENGINES
                    banks = run_halves(halves, engines, lambda: h_transposes(b - 1))
                    h_finish(b - 1, banks)
            norm_factor(b)
        cos_t, sin_t = load_rope_tables()

        delayed = {}
        for q in range(GROUPS):
            kind, idx = OUT_GROUPS[q]
            for b in range(BLOCKS):
                acc = acc_bank()
                for g in range(PASSES2):
                    mx_pass(acc, h_codes[b], weights[("b", q)], g, PASSES2 - 1)
                rows = slice(b * P, (b + 1) * P)
                if kind == "n":
                    o = u_tile()
                    nc.scalar.copy(out=o[:], in_=acc[:])
                    nc.sync.dma_start(
                        out=out_0[rows, 4 * idx : 4 * idx + 4, :], in_=o[:].rearrange("p (h d) -> p h d", d=NOPE)
                    )
                else:
                    a3 = acc[:].rearrange("p (h d) -> p h d", d=ROPE)
                    t1 = u_tile()
                    t2 = u_tile()
                    t13 = t1[:].rearrange("p (h d) -> p h d", d=ROPE)
                    t23 = t2[:].rearrange("p (h d) -> p h d", d=ROPE)
                    nc.vector.tensor_tensor(
                        out=t13, in0=a3, in1=cos_t[:, b : b + 1, :].to_broadcast([P, 8, ROPE]), op=ALU.mult
                    )
                    nc.vector.tensor_tensor(
                        out=t23[:, :, 0:HALF],
                        in0=a3[:, :, HALF:ROPE],
                        in1=sin_t[:, b : b + 1, 0:HALF].to_broadcast([P, 8, HALF]),
                        op=ALU.mult,
                    )
                    nc.vector.tensor_tensor(
                        out=t23[:, :, HALF:ROPE],
                        in0=a3[:, :, 0:HALF],
                        in1=sin_t[:, b : b + 1, HALF:ROPE].to_broadcast([P, 8, HALF]),
                        op=ALU.mult,
                    )
                    nc.gpsimd.tensor_tensor(out=t1[:], in0=t1[:], in1=t2[:], op=ALU.add)
                    nc.sync.dma_start(out=out_1[rows, 8 * idx : 8 * idx + 8, :], in_=t13)
                for quant in delayed.get(b, ()):
                    quant()
                delayed[b] = ()
                if q + 1 < GROUPS and b in WB_AT:
                    halves = wb_run(q + 1, WB_AT.index(b))
                    banks = None
                    if kind == "n":
                        halves[0][0](("V", "V"))
                        if q == 0 and b == WB_AT[0]:
                            banks = h_transposes(last)
                        halves[1][0](("V", "V"))
                        halves[0][1]()
                        halves[1][1]()
                    else:
                        halves[0][0](("S", "S"))
                        halves[1][0](("S", "S"))
                        delayed[b + 1] = (halves[0][1],)
                        delayed[b + 2] = (halves[1][1],)
                    if banks is not None:
                        h_finish(last, banks)
